import numpy as np
import ml_dtypes


def mxq(x, axis, fmt="e4m3"):
    dtype, down = {"e4m3": (ml_dtypes.float8_e4m3fn, 7), "e5m2": (ml_dtypes.float8_e5m2, 14)}[fmt]
    v = np.moveaxis(np.asarray(x, np.float32).astype(ml_dtypes.bfloat16).astype(np.float64), axis, -1)
    blocks = v.reshape(v.shape[:-1] + (-1, 32))
    amax = np.abs(blocks).max(-1, keepdims=True)
    byte = np.maximum(np.where(amax > 0, np.frexp(amax)[1] - 1 + 127, 0) - down, 1)
    scale = np.exp2(byte - 127.0)
    codes = (blocks / scale).astype(np.float32).astype(dtype).astype(np.float64)
    return np.moveaxis((codes * scale).reshape(v.shape), -1, axis)


WIDE = False


def mx_kscale(k):
    if not WIDE:
        return np.ones(k)
    levels = np.array([10, -10, 5, -5, 0])
    if k % 512:
        return np.exp2(np.random.permutation(np.resize(levels, k // 32))).repeat(32)
    a = np.empty((k // 512, 16))
    for p in range(k // 512):
        a[p, :8] = np.random.permutation(np.resize(levels, 8))
        for g in range(8):
            far = levels[np.abs(levels - a[p, g]) >= 10]
            a[p, g + 8] = far[np.random.randint(len(far))]
    return np.exp2(a.ravel()).repeat(32)


BF16 = ml_dtypes.bfloat16


def bf(x):
    return np.asarray(x, np.float32).astype(BF16)


def f64(x):
    return np.asarray(x).astype(np.float64)


B, S, H = 8, 49, 512
N = B * (S - 1)
G = 0.75


def setup_inputs():
    s = mx_kscale(H)
    return {"x": bf(np.random.standard_normal((B, S, H)) * s),
            "k1": bf(np.random.standard_normal((N, H)) * G * s),
            "k2": bf(np.random.standard_normal((N, H)) * G * np.sqrt(1.0 + 0.25 * G * G) * s),
            "coefficients": bf(np.random.standard_normal((H, H)) * G / np.sqrt(H) * s[:, None] / s[None, :])}


def reference(x, k1, k2, coefficients):
    x, k1, k2 = f64(x), f64(k1), f64(k2)
    y = x[:, :-1, :].reshape(-1, H)
    cq = mxq(f64(coefficients), 1, "e4m3")
    k3 = mxq(y + 0.5 * k2, 1, "e4m3") @ cq.T
    k4 = mxq(y + k3, 1, "e4m3") @ cq.T
    y1 = y + (k1 + 2.0 * k2 + 2.0 * k3 + k4) / 6.0
    return y1.reshape(B, S - 1, H) - x[:, 1:, :]

@@ -1,0 +1,187 @@
+from contextlib import ExitStack
+
+import concourse.mybir as mybir
+from concourse.masks import make_identity
+
+F32 = mybir.dt.float32
+BF16 = mybir.dt.bfloat16
+U32 = mybir.dt.uint32
+U8 = mybir.dt.uint8
+FP8X4 = mybir.dt.float8_e4m3fn_x4
+ALU = mybir.AluOpType
+COPY = mybir.ActivationFunctionType.Copy
+
+P = 128
+B = 8
+S = 49
+H = 512
+R = 3
+Q = (S - 1) // R
+PACK = 4
+HALF = 2
+
+FLOPS = 2 * 2 * B * (S - 1) * H * H
+
+
+def tile_sindylossmixin_pa_s_kernel(tc, x, k1, k2, coefficients, out):
+    nc = tc.nc
+    with ExitStack() as ctx:
+        keep = ctx.enter_context(tc.tile_pool(name="keep", bufs=1))
+        psum = ctx.enter_context(tc.psum_pool(name="psum", bufs=1))
+        ctx.enter_context(tc.manual_schedule())
+
+        x_sb = keep.tile([P, R + 1, H], BF16)
+        k1_sb = keep.tile([P, R, H], BF16)
+        k2_sb = keep.tile([P, R, H], BF16)
+        c_sb = keep.tile([P, PACK, H], BF16)
+        nc.sync.dma_start(
+            out=x_sb[:, 0:R, :].rearrange("p r h -> p (r h)"),
+            in_=x[:, 0 : S - 1, :].rearrange("b (q r) h -> q b (r h)", r=R),
+        )
+        nc.sync.dma_start(
+            out=x_sb[:, R, :],
+            in_=x[:, 1:S, :].rearrange("b (q r) h -> q b r h", r=R)[:, :, R - 1, :],
+        )
+        nc.sync.dma_start(
+            out=k2_sb[:].rearrange("p r h -> p (r h)"),
+            in_=k2.rearrange("(b q r) h -> q b (r h)", b=B, q=Q, r=R),
+        )
+        nc.sync.dma_start(
+            out=k1_sb[:].rearrange("p r h -> p (r h)"),
+            in_=k1.rearrange("(b q r) h -> q b (r h)", b=B, q=Q, r=R),
+        )
+        c_rows = coefficients.rearrange("(m t) j -> m t j", t=PACK)
+        for h in range(HALF):
+            nc.sync.dma_start(out=c_sb[:, HALF * h : HALF * (h + 1), :], in_=c_rows[:, HALF * h : HALF * (h + 1), :])
+
+        ident = keep.tile([P, P], F32)
+        make_identity(nc, ident[:])
+
+        warm = keep.tile([P, 2], F32)
+        nc.vector.memset(warm[:, 0:1], 0.0)
+        nc.scalar.activation(out=warm[:, 1:2], in_=warm[:, 0:1], func=COPY)
+
+        def transpose_words(bank, words):
+            for u in range(HALF):
+                nc.tensor.transpose(bank[:, u, :], words[:, u : HALF * P : HALF], ident[:])
+
+        x_words = x_sb[:].bitcast(F32)
+        k2_words = k2_sb[:].bitcast(F32)
+        c_words = c_sb[:].bitcast(F32)
+        yT = keep.tile([P, R, P, PACK], BF16, align_bytes=64)
+        half_k2T = keep.tile([P, R, P, PACK], BF16, align_bytes=64)
+        aT = keep.tile([P, R, P, PACK], BF16, align_bytes=64)
+        zT = keep.tile([P, R, P, PACK], BF16, align_bytes=64)
+        cT = keep.tile([P, H, PACK], BF16, align_bytes=64)
+        a_codes = keep.tile([P, R * P], U32, align_bytes=64)
+        a_scales = keep.tile([P, R * P], U8, align_bytes=64)
+        z_codes = keep.tile([P, R * P], U32, align_bytes=64)
+        z_scales = keep.tile([P, R * P], U8, align_bytes=64)
+        c_codes = keep.tile([P, H], U32, align_bytes=64)
+        c_scales = keep.tile([P, H], U8, align_bytes=64)
+        diff = keep.tile([P, R, H], F32)
+        k_sum = keep.tile([P, R, H], F32)
+        base = keep.tile([P, R, H], F32)
+        result = keep.tile([P, R, H], F32)
+
+        def quantise(codes, scales, cols, grouped):
+            nc.vector.quantize_mx(
+                out=codes[:, cols].bitcast(FP8X4), scales=scales[:, cols], in_=grouped
+            )
+
+        def chunk(r):
+            return slice(r * P, (r + 1) * P)
+
+        for r in range(R):
+            yT_ps = psum.tile([P, HALF, P], F32, tag="y_then_k3", bufs=R)
+            transpose_words(yT_ps, x_words[:, r, :])
+            nc.scalar.copy(
+                out=yT[:, r, :, :].bitcast(F32), in_=yT_ps[:].rearrange("p u n -> p n u")
+            )
+        nc.vector.tensor_tensor(
+            out=diff[:], in0=x_sb[:, 0:R, :], in1=x_sb[:, 1 : R + 1, :], op=ALU.subtract
+        )
+
+        for r in range(R):
+            k2T_ps = psum.tile([P, HALF, P], F32, tag="k2_then_sum", bufs=R)
+            transpose_words(k2T_ps, k2_words[:, r, :])
+            nc.scalar.activation(
+                out=half_k2T[:, r, :, :].rearrange("p n (u e) -> p n u e", e=HALF),
+                in_=k2T_ps[:].bitcast(BF16).rearrange("p u (n e) -> p n u e", e=HALF),
+                func=COPY,
+                scale=0.5,
+            )
+        nc.vector.scalar_tensor_tensor(
+            out=k_sum[:], in0=k2_sb[:], scalar=2.0, in1=k1_sb[:], op0=ALU.mult, op1=ALU.add
+        )
+        nc.vector.tensor_tensor(out=aT[:], in0=yT[:], in1=half_k2T[:], op=ALU.add)
+
+        for e in range(HALF):
+            cT_ps = psum.tile([P, HALF, HALF, P], F32, tag="c", bufs=HALF)
+            for u in range(HALF):
+                transpose_words(cT_ps[:, u, :, :], c_words[:, HALF * e + u, :])
+            cols = slice(e * HALF * P, (e + 1) * HALF * P)
+            nc.scalar.copy(
+                out=cT[:, cols, :].bitcast(F32).rearrange("p (u m) w -> p u m w", u=HALF),
+                in_=cT_ps[:].rearrange("p u w m -> p u m w"),
+            )
+        half_cols = [slice(e * HALF * P, (e + 1) * HALF * P) for e in range(HALF)]
+        quantise(c_codes, c_scales, half_cols[0], cT[:, half_cols[0], :].rearrange("p i t -> p (i t)"))
+        for r in range(R):
+            quantise(a_codes, a_scales, chunk(r), aT[:, r, :, :].rearrange("p n t -> p (n t)"))
+        quantise(c_codes, c_scales, half_cols[1], cT[:, half_cols[1], :].rearrange("p i t -> p (i t)"))
+        nc.vector.scalar_tensor_tensor(
+            out=base[:], in0=k_sum[:], scalar=1.0 / 6.0, in1=diff[:], op0=ALU.mult, op1=ALU.add
+        )
+
+        k3T_banks = []
+        for r in range(R):
+            k3T_ps = psum.tile([P, PACK, P], F32, tag="y_then_k3", bufs=R)
+            k3T_banks.append(k3T_ps)
+            for g in range(PACK):
+                nc.tensor.matmul_mx(
+                    out=k3T_ps[:, g, :],
+                    lhsT=c_codes[:, chunk(g)].bitcast(FP8X4),
+                    lhsT_scale=c_scales[:, chunk(g)],
+                    rhs=a_codes[:, chunk(r)].bitcast(FP8X4),
+                    rhs_scale=a_scales[:, chunk(r)],
+                    start=True,
+                    stop=True,
+                )
+
+        for r in range(R + 1):
+            if r < R:
+                nc.vector.tensor_tensor(
+                    out=zT[:, r, :, :],
+                    in0=k3T_banks[r][:].rearrange("p t n -> p n t"),
+                    in1=yT[:, r, :, :],
+                    op=ALU.add,
+                )
+            if r > 0:
+                quantise(
+                    z_codes, z_scales, chunk(r - 1), zT[:, r - 1, :, :].rearrange("p n t -> p (n t)")
+                )
+
+        out_rows = out.rearrange("b (q r) h -> q b r h", r=R)
+        for r in range(R):
+            sum_ps = psum.tile([P, H], F32, tag="k2_then_sum", bufs=R)
+            passes = [(a_codes, a_scales), (a_codes, a_scales), (z_codes, z_scales)]
+            for n_pass, (codes, scales) in enumerate(passes):
+                nc.tensor.matmul_mx(
+                    out=sum_ps[:],
+                    lhsT=codes[:, chunk(r)].bitcast(FP8X4),
+                    lhsT_scale=scales[:, chunk(r)],
+                    rhs=c_codes[:].bitcast(FP8X4),
+                    rhs_scale=c_scales[:],
+                    start=(n_pass == 0),
+                    stop=(n_pass == len(passes) - 1),
+                )
+            nc.vector.scalar_tensor_tensor(
+                out=result[:, r, :].rearrange("p (m t) -> p m t", t=PACK),
+                in0=sum_ps[:].rearrange("p (t m) -> p m t", t=PACK),
+                scalar=1.0 / 6.0,
+                in1=base[:, r, :].rearrange("p (m t) -> p m t", t=PACK),
+                op0=ALU.mult,
+                op1=ALU.add,
+            )
+            nc.sync.dma_start(out=out_rows[:, :, r, :], in_=result[:, r, :])

@@ -18,6 +18,7 @@ H = 512
 R = 3
 Q = (S - 1) // R
 PACK = 4
+W = H // 2
 HALF = 2
 
 FLOPS = 2 * 2 * B * (S - 1) * H * H
@@ -46,13 +47,16 @@ def tile_sindylossmixin_pa_s_kernel(tc, x, k1, k2, coefficients, out):
             out=k2_sb[:].rearrange("p r h -> p (r h)"),
             in_=k2.rearrange("(b q r) h -> q b (r h)", b=B, q=Q, r=R),
         )
+        c_rows = coefficients.rearrange("(m t) j -> m t j", t=PACK)
+        for h in range(HALF):
+            nc.sync.dma_start(
+                out=c_sb[:, HALF * h : HALF * (h + 1), :],
+                in_=c_rows[:, HALF * h : HALF * (h + 1), :],
+            )
         nc.sync.dma_start(
             out=k1_sb[:].rearrange("p r h -> p (r h)"),
             in_=k1.rearrange("(b q r) h -> q b (r h)", b=B, q=Q, r=R),
         )
-        c_rows = coefficients.rearrange("(m t) j -> m t j", t=PACK)
-        for h in range(HALF):
-            nc.sync.dma_start(out=c_sb[:, HALF * h : HALF * (h + 1), :], in_=c_rows[:, HALF * h : HALF * (h + 1), :])
 
         ident = keep.tile([P, P], F32)
         make_identity(nc, ident[:])
@@ -61,15 +65,29 @@ def tile_sindylossmixin_pa_s_kernel(tc, x, k1, k2, coefficients, out):
         nc.vector.memset(warm[:, 0:1], 0.0)
         nc.scalar.activation(out=warm[:, 1:2], in_=warm[:, 0:1], func=COPY)
 
+        weights = [6.0, -6.0, 2.0, 1.0]
+        scaled_ident = keep.tile([P, len(weights), P], BF16, align_bytes=64)
+        for i, weight in enumerate(weights):
+            nc.scalar.activation(out=scaled_ident[:, i, :], in_=ident[:], func=COPY, scale=weight)
+
+        def new_bank():
+            bank = psum.tile([P, H], F32, tag="bank", bufs=8)
+            return bank
+
         def transpose_words(bank, words):
             for u in range(HALF):
-                nc.tensor.transpose(bank[:, u, :], words[:, u : HALF * P : HALF], ident[:])
+                nc.tensor.transpose(bank[:, u * P : (u + 1) * P], words[:, u : HALF * P : HALF], ident[:])
+
+        def by_row(bank):
+            return bank[:, 0 : HALF * P].bitcast(BF16).rearrange("p (u n e) -> p n u e", u=HALF, e=HALF)
+
+        def in_pairs(grouped):
+            return grouped.rearrange("p n (u e) -> p n u e", e=HALF)
 
         x_words = x_sb[:].bitcast(F32)
         k2_words = k2_sb[:].bitcast(F32)
         c_words = c_sb[:].bitcast(F32)
-        yT = keep.tile([P, R, P, PACK], BF16, align_bytes=64)
-        half_k2T = keep.tile([P, R, P, PACK], BF16, align_bytes=64)
+        y2T = keep.tile([P, R, P, PACK], BF16, align_bytes=64)
         aT = keep.tile([P, R, P, PACK], BF16, align_bytes=64)
         zT = keep.tile([P, R, P, PACK], BF16, align_bytes=64)
         cT = keep.tile([P, H, PACK], BF16, align_bytes=64)
@@ -79,70 +97,79 @@ def tile_sindylossmixin_pa_s_kernel(tc, x, k1, k2, coefficients, out):
         z_scales = keep.tile([P, R * P], U8, align_bytes=64)
         c_codes = keep.tile([P, H], U32, align_bytes=64)
         c_scales = keep.tile([P, H], U8, align_bytes=64)
-        diff = keep.tile([P, R, H], F32)
-        k_sum = keep.tile([P, R, H], F32)
         base = keep.tile([P, R, H], F32)
         result = keep.tile([P, R, H], F32)
 
         def quantise(codes, scales, cols, grouped):
             nc.vector.quantize_mx(
-                out=codes[:, cols].bitcast(FP8X4), scales=scales[:, cols], in_=grouped
+                out=codes[:, cols].bitcast(FP8X4),
+                scales=scales[:, cols],
+                in_=grouped.rearrange("p n t -> p (n t)"),
             )
 
         def chunk(r):
             return slice(r * P, (r + 1) * P)
 
         for r in range(R):
-            yT_ps = psum.tile([P, HALF, P], F32, tag="y_then_k3", bufs=R)
-            transpose_words(yT_ps, x_words[:, r, :])
-            nc.scalar.copy(
-                out=yT[:, r, :, :].bitcast(F32), in_=yT_ps[:].rearrange("p u n -> p n u")
-            )
+            bank = new_bank()
+            transpose_words(bank, x_words[:, r, :])
+            nc.scalar.activation(out=in_pairs(y2T[:, r, :, :]), in_=by_row(bank), func=COPY, scale=2.0)
         nc.vector.tensor_tensor(
-            out=diff[:], in0=x_sb[:, 0:R, :], in1=x_sb[:, 1 : R + 1, :], op=ALU.subtract
+            out=base[:, 0 : R - 1, :], in0=x_sb[:, 0 : R - 1, :], in1=x_sb[:, 1:R, :], op=ALU.subtract
         )
+        nc.vector.tensor_tensor(
+            out=base[:, R - 1, 0:W], in0=x_sb[:, R - 1, 0:W], in1=x_sb[:, R, 0:W], op=ALU.subtract
+        )
+
+        def add_stage(r, stage, factor):
+            cols = slice(0, H if r < R - 1 else W)
+            nc.vector.scalar_tensor_tensor(
+                out=base[:, r, cols], in0=stage[:, r, cols], scalar=factor, in1=base[:, r, cols],
+                op0=ALU.mult, op1=ALU.add,
+            )
+
+        add_stage(0, k2_sb, 1.0 / 3.0)
 
         for r in range(R):
-            k2T_ps = psum.tile([P, HALF, P], F32, tag="k2_then_sum", bufs=R)
-            transpose_words(k2T_ps, k2_words[:, r, :])
-            nc.scalar.activation(
-                out=half_k2T[:, r, :, :].rearrange("p n (u e) -> p n u e", e=HALF),
-                in_=k2T_ps[:].bitcast(BF16).rearrange("p u (n e) -> p n u e", e=HALF),
-                func=COPY,
-                scale=0.5,
+            bank = new_bank()
+            transpose_words(bank, k2_words[:, r, :])
+            nc.vector.tensor_tensor(
+                out=in_pairs(aT[:, r, :, :]), in0=by_row(bank), in1=in_pairs(y2T[:, r, :, :]), op=ALU.add
             )
-        nc.vector.scalar_tensor_tensor(
-            out=k_sum[:], in0=k2_sb[:], scalar=2.0, in1=k1_sb[:], op0=ALU.mult, op1=ALU.add
-        )
-        nc.vector.tensor_tensor(out=aT[:], in0=yT[:], in1=half_k2T[:], op=ALU.add)
 
-        for e in range(HALF):
-            cT_ps = psum.tile([P, HALF, HALF, P], F32, tag="c", bufs=HALF)
-            for u in range(HALF):
-                transpose_words(cT_ps[:, u, :, :], c_words[:, HALF * e + u, :])
-            cols = slice(e * HALF * P, (e + 1) * HALF * P)
+        for t in range(PACK):
+            bank = new_bank()
+            transpose_words(bank, c_words[:, t, :])
             nc.scalar.copy(
-                out=cT[:, cols, :].bitcast(F32).rearrange("p (u m) w -> p u m w", u=HALF),
-                in_=cT_ps[:].rearrange("p u w m -> p u m w"),
+                out=cT[:, chunk(t), :].bitcast(F32),
+                in_=bank[:, 0 : HALF * P].rearrange("p (u m) -> p m u", u=HALF),
             )
-        half_cols = [slice(e * HALF * P, (e + 1) * HALF * P) for e in range(HALF)]
-        quantise(c_codes, c_scales, half_cols[0], cT[:, half_cols[0], :].rearrange("p i t -> p (i t)"))
+
+        bank = new_bank()
+        rows = [x_sb[:, R - 1, W:H], x_sb[:, R, W:H], k2_sb[:, R - 1, W:H], k1_sb[:, R - 1, W:H]]
+        for i, row in enumerate(rows):
+            nc.tensor.matmul(
+                bank[:, 0:W], scaled_ident[:, i, :], row, start=(i == 0), stop=(i == len(rows) - 1)
+            )
+        nc.scalar.activation(out=base[:, R - 1, W:H], in_=bank[:, 0:W], func=COPY, scale=1.0 / 6.0)
+
         for r in range(R):
-            quantise(a_codes, a_scales, chunk(r), aT[:, r, :, :].rearrange("p n t -> p (n t)"))
-        quantise(c_codes, c_scales, half_cols[1], cT[:, half_cols[1], :].rearrange("p i t -> p (i t)"))
-        nc.vector.scalar_tensor_tensor(
-            out=base[:], in0=k_sum[:], scalar=1.0 / 6.0, in1=diff[:], op0=ALU.mult, op1=ALU.add
-        )
+            quantise(a_codes, a_scales, chunk(r), aT[:, r, :, :])
+        quantise(c_codes, c_scales, slice(0, 2 * P), cT[:, 0 : 2 * P, :])
+        quantise(c_codes, c_scales, chunk(2), cT[:, chunk(2), :])
+        quantise(c_codes, c_scales, chunk(3), cT[:, chunk(3), :])
+        add_stage(1, k2_sb, 1.0 / 3.0)
 
         k3T_banks = []
         for r in range(R):
-            k3T_ps = psum.tile([P, PACK, P], F32, tag="y_then_k3", bufs=R)
-            k3T_banks.append(k3T_ps)
-            for g in range(PACK):
+            bank = new_bank()
+            k3T_banks.append(bank)
+        for t in range(PACK):
+            for r in range(R):
                 nc.tensor.matmul_mx(
-                    out=k3T_ps[:, g, :],
-                    lhsT=c_codes[:, chunk(g)].bitcast(FP8X4),
-                    lhsT_scale=c_scales[:, chunk(g)],
+                    out=k3T_banks[r][:, chunk(t)],
+                    lhsT=c_codes[:, chunk(t)].bitcast(FP8X4),
+                    lhsT_scale=c_scales[:, chunk(t)],
                     rhs=a_codes[:, chunk(r)].bitcast(FP8X4),
                     rhs_scale=a_scales[:, chunk(r)],
                     start=True,
@@ -153,35 +180,54 @@ def tile_sindylossmixin_pa_s_kernel(tc, x, k1, k2, coefficients, out):
             if r < R:
                 nc.vector.tensor_tensor(
                     out=zT[:, r, :, :],
-                    in0=k3T_banks[r][:].rearrange("p t n -> p n t"),
-                    in1=yT[:, r, :, :],
+                    in0=k3T_banks[r][:].rearrange("p (t n) -> p n t", t=PACK),
+                    in1=y2T[:, r, :, :],
                     op=ALU.add,
                 )
+            if r == R:
+                add_stage(2, k2_sb, 1.0 / 3.0)
             if r > 0:
-                quantise(
-                    z_codes, z_scales, chunk(r - 1), zT[:, r - 1, :, :].rearrange("p n t -> p (n t)")
-                )
+                quantise(z_codes, z_scales, chunk(r - 1), zT[:, r - 1, :, :])
+
+        def pass_over(bank, codes, scales, r, start, stop):
+            nc.tensor.matmul_mx(
+                out=bank[:],
+                lhsT=codes[:, chunk(r)].bitcast(FP8X4),
+                lhsT_scale=scales[:, chunk(r)],
+                rhs=c_codes[:].bitcast(FP8X4),
+                rhs_scale=c_scales[:],
+                start=start,
+                stop=stop,
+            )
+
+        sum_banks = []
+        for r in range(R):
+            bank = new_bank()
+            sum_banks.append(bank)
+            pass_over(bank, a_codes, a_scales, r, True, False)
+            pass_over(bank, a_codes, a_scales, r, False, False)
+        for r in range(R):
+            pass_over(sum_banks[r], z_codes, z_scales, r, False, True)
 
         out_rows = out.rearrange("b (q r) h -> q b r h", r=R)
-        for r in range(R):
-            sum_ps = psum.tile([P, H], F32, tag="k2_then_sum", bufs=R)
-            passes = [(a_codes, a_scales), (a_codes, a_scales), (z_codes, z_scales)]
-            for n_pass, (codes, scales) in enumerate(passes):
-                nc.tensor.matmul_mx(
-                    out=sum_ps[:],
-                    lhsT=codes[:, chunk(r)].bitcast(FP8X4),
-                    lhsT_scale=scales[:, chunk(r)],
-                    rhs=c_codes[:].bitcast(FP8X4),
-                    rhs_scale=c_scales[:],
-                    start=(n_pass == 0),
-                    stop=(n_pass == len(passes) - 1),
-                )
+
+        def finish(r, cols):
             nc.vector.scalar_tensor_tensor(
-                out=result[:, r, :].rearrange("p (m t) -> p m t", t=PACK),
-                in0=sum_ps[:].rearrange("p (t m) -> p m t", t=PACK),
-                scalar=1.0 / 6.0,
-                in1=base[:, r, :].rearrange("p (m t) -> p m t", t=PACK),
+                out=result[:, r, cols].rearrange("p (m t) -> p m t", t=PACK),
+                in0=sum_banks[r][:].rearrange("p (t m) -> p m t", t=PACK)[
+                    :, cols.start // PACK : cols.stop // PACK, :
+                ],
+                scalar=1.0 / 12.0,
+                in1=base[:, r, cols].rearrange("p (m t) -> p m t", t=PACK),
                 op0=ALU.mult,
                 op1=ALU.add,
             )
-            nc.sync.dma_start(out=out_rows[:, :, r, :], in_=result[:, r, :])
+            nc.sync.dma_start(out=out_rows[:, :, r, cols], in_=result[:, r, cols])
+
+        add_stage(0, k1_sb, 1.0 / 6.0)
+        add_stage(1, k1_sb, 1.0 / 6.0)
+        finish(0, slice(0, H))
+        add_stage(2, k1_sb, 1.0 / 6.0)
+        finish(1, slice(0, H))
+        finish(2, slice(0, W))
+        finish(2, slice(W, H))

@@ -35,14 +35,13 @@ def tile_sindylossmixin_pa_s_kernel(tc, x, k1, k2, coefficients, out):
         k1_sb = keep.tile([P, R, H], BF16)
         k2_sb = keep.tile([P, R, H], BF16)
         c_sb = keep.tile([P, PACK, H], BF16)
-        nc.sync.dma_start(
-            out=x_sb[:, 0:R, :].rearrange("p r h -> p (r h)"),
-            in_=x[:, 0 : S - 1, :].rearrange("b (q r) h -> q b (r h)", r=R),
-        )
-        nc.sync.dma_start(
-            out=x_sb[:, R, :],
-            in_=x[:, 1:S, :].rearrange("b (q r) h -> q b r h", r=R)[:, :, R - 1, :],
-        )
+        for first in (0, 2):
+            nc.sync.dma_start(
+                out=x_sb[:, first : first + 2, :].rearrange("p r h -> p (r h)"),
+                in_=x[:, first // 2 : first // 2 + S - 1, :].rearrange("b (q r) h -> q b (r h)", r=R)[
+                    :, :, first // 2 * H : (first // 2 + 2) * H
+                ],
+            )
         nc.sync.dma_start(
             out=k2_sb[:].rearrange("p r h -> p (r h)"),
             in_=k2.rearrange("(b q r) h -> q b (r h)", b=B, q=Q, r=R),
@@ -99,6 +98,7 @@ def tile_sindylossmixin_pa_s_kernel(tc, x, k1, k2, coefficients, out):
         c_scales = keep.tile([P, H], U8, align_bytes=64)
         base = keep.tile([P, R, H], F32)
         result = keep.tile([P, R, H], F32)
+        k1_sixth = keep.tile([P, H + W], F32)
 
         def quantise(codes, scales, cols, grouped):
             nc.vector.quantize_mx(
@@ -114,12 +114,11 @@ def tile_sindylossmixin_pa_s_kernel(tc, x, k1, k2, coefficients, out):
             bank = new_bank()
             transpose_words(bank, x_words[:, r, :])
             nc.scalar.activation(out=in_pairs(y2T[:, r, :, :]), in_=by_row(bank), func=COPY, scale=2.0)
-        nc.vector.tensor_tensor(
-            out=base[:, 0 : R - 1, :], in0=x_sb[:, 0 : R - 1, :], in1=x_sb[:, 1:R, :], op=ALU.subtract
-        )
-        nc.vector.tensor_tensor(
-            out=base[:, R - 1, 0:W], in0=x_sb[:, R - 1, 0:W], in1=x_sb[:, R, 0:W], op=ALU.subtract
-        )
+        for r in range(R):
+            cols = slice(0, H if r < R - 1 else W)
+            nc.vector.tensor_tensor(
+                out=base[:, r, cols], in0=x_sb[:, r, cols], in1=x_sb[:, r + 1, cols], op=ALU.subtract
+            )
 
         def add_stage(r, stage, factor):
             cols = slice(0, H if r < R - 1 else W)
@@ -152,6 +151,16 @@ def tile_sindylossmixin_pa_s_kernel(tc, x, k1, k2, coefficients, out):
                 bank[:, 0:W], scaled_ident[:, i, :], row, start=(i == 0), stop=(i == len(rows) - 1)
             )
         nc.scalar.activation(out=base[:, R - 1, W:H], in_=bank[:, 0:W], func=COPY, scale=1.0 / 6.0)
+        nc.scalar.activation(out=k1_sixth[:, 0:H], in_=k1_sb[:, 1, :], func=COPY, scale=1.0 / 6.0)
+        nc.scalar.activation(
+            out=k1_sixth[:, H : H + W], in_=k1_sb[:, R - 1, 0:W], func=COPY, scale=1.0 / 6.0
+        )
+
+        def add_k1_on_gpsimd(r, cols):
+            scaled = k1_sixth[:, (r - 1) * H + cols.start : (r - 1) * H + cols.stop]
+            nc.gpsimd.tensor_tensor(
+                out=base[:, r, cols], in0=base[:, r, cols], in1=scaled, op=ALU.add
+            )
 
         for r in range(R):
             quantise(a_codes, a_scales, chunk(r), aT[:, r, :, :])
@@ -159,6 +168,8 @@ def tile_sindylossmixin_pa_s_kernel(tc, x, k1, k2, coefficients, out):
         quantise(c_codes, c_scales, chunk(2), cT[:, chunk(2), :])
         quantise(c_codes, c_scales, chunk(3), cT[:, chunk(3), :])
         add_stage(1, k2_sb, 1.0 / 3.0)
+        add_k1_on_gpsimd(1, slice(0, W))
+        add_k1_on_gpsimd(1, slice(W, H))
 
         k3T_banks = []
         for r in range(R):
@@ -185,7 +196,7 @@ def tile_sindylossmixin_pa_s_kernel(tc, x, k1, k2, coefficients, out):
                     op=ALU.add,
                 )
             if r == R:
-                add_stage(2, k2_sb, 1.0 / 3.0)
+                add_stage(0, k1_sb, 1.0 / 6.0)
             if r > 0:
                 quantise(z_codes, z_scales, chunk(r - 1), zT[:, r - 1, :, :])
 
@@ -224,10 +235,9 @@ def tile_sindylossmixin_pa_s_kernel(tc, x, k1, k2, coefficients, out):
             )
             nc.sync.dma_start(out=out_rows[:, :, r, cols], in_=result[:, r, cols])
 
-        add_stage(0, k1_sb, 1.0 / 6.0)
-        add_stage(1, k1_sb, 1.0 / 6.0)
+        add_stage(2, k2_sb, 1.0 / 3.0)
+        add_k1_on_gpsimd(2, slice(0, W))
         finish(0, slice(0, H))
-        add_stage(2, k1_sb, 1.0 / 6.0)
         finish(1, slice(0, H))
         finish(2, slice(0, W))
         finish(2, slice(W, H))

@@ -18,7 +18,7 @@ H = 512
 R = 3
 Q = (S - 1) // R
 PACK = 4
-W = H // 2
+W = 208
 HALF = 2
 
 FLOPS = 2 * 2 * B * (S - 1) * H * H
@@ -98,7 +98,8 @@ def tile_sindylossmixin_pa_s_kernel(tc, x, k1, k2, coefficients, out):
         c_scales = keep.tile([P, H], U8, align_bytes=64)
         base = keep.tile([P, R, H], F32)
         result = keep.tile([P, R, H], F32)
-        k1_sixth = keep.tile([P, H + W], F32)
+        k1_sixth = keep.tile([P, R, H], F32)
+        stages = keep.tile([P, H // 2], F32)
 
         def quantise(codes, scales, cols, grouped):
             nc.vector.quantize_mx(
@@ -120,14 +121,13 @@ def tile_sindylossmixin_pa_s_kernel(tc, x, k1, k2, coefficients, out):
                 out=base[:, r, cols], in0=x_sb[:, r, cols], in1=x_sb[:, r + 1, cols], op=ALU.subtract
             )
 
-        def add_stage(r, stage, factor):
-            cols = slice(0, H if r < R - 1 else W)
+        def add_stage(r, cols, stage, factor):
             nc.vector.scalar_tensor_tensor(
                 out=base[:, r, cols], in0=stage[:, r, cols], scalar=factor, in1=base[:, r, cols],
                 op0=ALU.mult, op1=ALU.add,
             )
 
-        add_stage(0, k2_sb, 1.0 / 3.0)
+        add_stage(0, slice(0, H), k2_sb, 1.0 / 3.0)
 
         for r in range(R):
             bank = new_bank()
@@ -148,18 +148,21 @@ def tile_sindylossmixin_pa_s_kernel(tc, x, k1, k2, coefficients, out):
         rows = [x_sb[:, R - 1, W:H], x_sb[:, R, W:H], k2_sb[:, R - 1, W:H], k1_sb[:, R - 1, W:H]]
         for i, row in enumerate(rows):
             nc.tensor.matmul(
-                bank[:, 0:W], scaled_ident[:, i, :], row, start=(i == 0), stop=(i == len(rows) - 1)
+                bank[:, 0 : H - W], scaled_ident[:, i, :], row, start=(i == 0), stop=(i == len(rows) - 1)
             )
-        nc.scalar.activation(out=base[:, R - 1, W:H], in_=bank[:, 0:W], func=COPY, scale=1.0 / 6.0)
-        nc.scalar.activation(out=k1_sixth[:, 0:H], in_=k1_sb[:, 1, :], func=COPY, scale=1.0 / 6.0)
-        nc.scalar.activation(
-            out=k1_sixth[:, H : H + W], in_=k1_sb[:, R - 1, 0:W], func=COPY, scale=1.0 / 6.0
-        )
+        nc.scalar.activation(out=base[:, R - 1, W:H], in_=bank[:, 0 : H - W], func=COPY, scale=1.0 / 6.0)
+        everything = slice(0, H)
+        left = slice(0, H // 2)
+        right = slice(H // 2, H)
+        own = slice(0, W)
+        for r, cols in ((1, everything), (0, right), (2, own)):
+            nc.scalar.activation(
+                out=k1_sixth[:, r, cols], in_=k1_sb[:, r, cols], func=COPY, scale=1.0 / 6.0
+            )
 
         def add_k1_on_gpsimd(r, cols):
-            scaled = k1_sixth[:, (r - 1) * H + cols.start : (r - 1) * H + cols.stop]
             nc.gpsimd.tensor_tensor(
-                out=base[:, r, cols], in0=base[:, r, cols], in1=scaled, op=ALU.add
+                out=base[:, r, cols], in0=base[:, r, cols], in1=k1_sixth[:, r, cols], op=ALU.add
             )
 
         for r in range(R):
@@ -167,9 +170,10 @@ def tile_sindylossmixin_pa_s_kernel(tc, x, k1, k2, coefficients, out):
         quantise(c_codes, c_scales, slice(0, 2 * P), cT[:, 0 : 2 * P, :])
         quantise(c_codes, c_scales, chunk(2), cT[:, chunk(2), :])
         quantise(c_codes, c_scales, chunk(3), cT[:, chunk(3), :])
-        add_stage(1, k2_sb, 1.0 / 3.0)
-        add_k1_on_gpsimd(1, slice(0, W))
-        add_k1_on_gpsimd(1, slice(W, H))
+        add_stage(1, everything, k2_sb, 1.0 / 3.0)
+        add_k1_on_gpsimd(1, left)
+        add_k1_on_gpsimd(1, right)
+        add_k1_on_gpsimd(0, right)
 
         k3T_banks = []
         for r in range(R):
@@ -195,8 +199,10 @@ def tile_sindylossmixin_pa_s_kernel(tc, x, k1, k2, coefficients, out):
                     in1=y2T[:, r, :, :],
                     op=ALU.add,
                 )
+            if r == R - 1:
+                add_stage(0, left, k1_sb, 1.0 / 6.0)
             if r == R:
-                add_stage(0, k1_sb, 1.0 / 6.0)
+                add_stage(2, own, k2_sb, 1.0 / 3.0)
             if r > 0:
                 quantise(z_codes, z_scales, chunk(r - 1), zT[:, r - 1, :, :])
 
@@ -222,22 +228,36 @@ def tile_sindylossmixin_pa_s_kernel(tc, x, k1, k2, coefficients, out):
 
         out_rows = out.rearrange("b (q r) h -> q b r h", r=R)
 
+        def by_component(cols):
+            return slice(cols.start // PACK, cols.stop // PACK)
+
+        def sums(r, cols):
+            return sum_banks[r][:].rearrange("p (t m) -> p m t", t=PACK)[:, by_component(cols), :]
+
         def finish(r, cols):
             nc.vector.scalar_tensor_tensor(
                 out=result[:, r, cols].rearrange("p (m t) -> p m t", t=PACK),
-                in0=sum_banks[r][:].rearrange("p (t m) -> p m t", t=PACK)[
-                    :, cols.start // PACK : cols.stop // PACK, :
-                ],
+                in0=sums(r, cols),
                 scalar=1.0 / 12.0,
                 in1=base[:, r, cols].rearrange("p (m t) -> p m t", t=PACK),
                 op0=ALU.mult,
                 op1=ALU.add,
             )
-            nc.sync.dma_start(out=out_rows[:, :, r, cols], in_=result[:, r, cols])
 
-        add_stage(2, k2_sb, 1.0 / 3.0)
-        add_k1_on_gpsimd(2, slice(0, W))
-        finish(0, slice(0, H))
-        finish(1, slice(0, H))
-        finish(2, slice(0, W))
+        def store(queue, r, cols):
+            queue.dma_start(out=out_rows[:, :, r, cols], in_=result[:, r, cols])
+
+        nc.scalar.activation(
+            out=stages[:].rearrange("p (m t) -> p m t", t=PACK), in_=sums(0, right), func=COPY, scale=1.0 / 12.0
+        )
+        add_k1_on_gpsimd(2, own)
+        nc.gpsimd.tensor_tensor(out=result[:, 0, right], in0=stages[:], in1=base[:, 0, right], op=ALU.add)
+        finish(0, left)
+        store(nc.sync, 0, left)
+        finish(1, everything)
+        store(nc.sync, 1, everything)
         finish(2, slice(W, H))
+        store(nc.sync, 2, slice(W, H))
+        store(nc.scalar, 0, right)
+        finish(2, own)
+        store(nc.sync, 2, own)

@@ -69,8 +69,8 @@ def tile_sindylossmixin_pa_s_kernel(tc, x, k1, k2, coefficients, out):
         for i, weight in enumerate(weights):
             nc.scalar.activation(out=scaled_ident[:, i, :], in_=ident[:], func=COPY, scale=weight)
 
-        def new_bank():
-            bank = psum.tile([P, H], F32, tag="bank", bufs=8)
+        def new_bank(number):
+            bank = psum.tile([P, H], F32, tag="bank%d" % number, bufs=1)
             return bank
 
         def transpose_words(bank, words):
@@ -112,7 +112,7 @@ def tile_sindylossmixin_pa_s_kernel(tc, x, k1, k2, coefficients, out):
             return slice(r * P, (r + 1) * P)
 
         for r in range(R):
-            bank = new_bank()
+            bank = new_bank(r)
             transpose_words(bank, x_words[:, r, :])
             nc.scalar.activation(out=in_pairs(y2T[:, r, :, :]), in_=by_row(bank), func=COPY, scale=2.0)
         for r in range(R):
@@ -130,27 +130,31 @@ def tile_sindylossmixin_pa_s_kernel(tc, x, k1, k2, coefficients, out):
         add_stage(0, slice(0, H), k2_sb, 1.0 / 3.0)
 
         for r in range(R):
-            bank = new_bank()
+            bank = new_bank(4 + r)
             transpose_words(bank, k2_words[:, r, :])
             nc.vector.tensor_tensor(
                 out=in_pairs(aT[:, r, :, :]), in0=by_row(bank), in1=in_pairs(y2T[:, r, :, :]), op=ALU.add
             )
 
         for t in range(PACK):
-            bank = new_bank()
+            bank = new_bank([7, 0, 1, 2][t])
             transpose_words(bank, c_words[:, t, :])
             nc.scalar.copy(
                 out=cT[:, chunk(t), :].bitcast(F32),
                 in_=bank[:, 0 : HALF * P].rearrange("p (u m) -> p m u", u=HALF),
             )
 
-        bank = new_bank()
+        known_bank = new_bank(3)
         rows = [x_sb[:, R - 1, W:H], x_sb[:, R, W:H], k2_sb[:, R - 1, W:H], k1_sb[:, R - 1, W:H]]
-        for i, row in enumerate(rows):
+
+        def add_on_tensor(i):
             nc.tensor.matmul(
-                bank[:, 0 : H - W], scaled_ident[:, i, :], row, start=(i == 0), stop=(i == len(rows) - 1)
+                known_bank[:, 0 : H - W], scaled_ident[:, i, :], rows[i],
+                start=(i == 0), stop=(i == len(rows) - 1),
             )
-        nc.scalar.activation(out=base[:, R - 1, W:H], in_=bank[:, 0 : H - W], func=COPY, scale=1.0 / 6.0)
+
+        for i in range(len(rows) - 1):
+            add_on_tensor(i)
         everything = slice(0, H)
         left = slice(0, H // 2)
         right = slice(H // 2, H)
@@ -177,10 +181,9 @@ def tile_sindylossmixin_pa_s_kernel(tc, x, k1, k2, coefficients, out):
 
         k3T_banks = []
         for r in range(R):
-            bank = new_bank()
+            bank = new_bank(4 + r)
             k3T_banks.append(bank)
-        for t in range(PACK):
-            for r in range(R):
+            for t in range(PACK):
                 nc.tensor.matmul_mx(
                     out=k3T_banks[r][:, chunk(t)],
                     lhsT=c_codes[:, chunk(t)].bitcast(FP8X4),
@@ -190,6 +193,11 @@ def tile_sindylossmixin_pa_s_kernel(tc, x, k1, k2, coefficients, out):
                     start=True,
                     stop=True,
                 )
+
+        add_on_tensor(len(rows) - 1)
+        nc.scalar.activation(
+            out=base[:, R - 1, W:H], in_=known_bank[:, 0 : H - W], func=COPY, scale=1.0 / 6.0
+        )
 
         for r in range(R + 1):
             if r < R:
@@ -219,12 +227,11 @@ def tile_sindylossmixin_pa_s_kernel(tc, x, k1, k2, coefficients, out):
 
         sum_banks = []
         for r in range(R):
-            bank = new_bank()
+            bank = new_bank([7, 0, 1][r])
             sum_banks.append(bank)
             pass_over(bank, a_codes, a_scales, r, True, False)
             pass_over(bank, a_codes, a_scales, r, False, False)
-        for r in range(R):
-            pass_over(sum_banks[r], z_codes, z_scales, r, False, True)
+            pass_over(bank, z_codes, z_scales, r, False, True)
 
         out_rows = out.rearrange("b (q r) h -> q b r h", r=R)
 

@@ -18,7 +18,7 @@ H = 512
 R = 3
 Q = (S - 1) // R
 PACK = 4
-W = 208
+W = 384
 HALF = 2
 
 FLOPS = 2 * 2 * B * (S - 1) * H * H
@@ -57,6 +57,10 @@ def tile_sindylossmixin_pa_s_kernel(tc, x, k1, k2, coefficients, out):
             in_=k1.rearrange("(b q r) h -> q b (r h)", b=B, q=Q, r=R),
         )
 
+        def new_bank(number):
+            bank = psum.tile([P, H], F32, tag="bank%d" % number, bufs=1)
+            return bank
+
         ident = keep.tile([P, P], F32)
         make_identity(nc, ident[:])
 
@@ -64,14 +68,18 @@ def tile_sindylossmixin_pa_s_kernel(tc, x, k1, k2, coefficients, out):
         nc.vector.memset(warm[:, 0:1], 0.0)
         nc.scalar.activation(out=warm[:, 1:2], in_=warm[:, 0:1], func=COPY)
 
+        idle_bank = new_bank(3)
+
+        def multiply_idly(count, columns):
+            for i in range(count):
+                nc.tensor.matmul(idle_bank[:, 0:columns], ident[:], ident[:, 0:columns], start=True, stop=True)
+
+        multiply_idly(4, 112)
+
         weights = [6.0, -6.0, 2.0, 1.0]
         scaled_ident = keep.tile([P, len(weights), P], BF16, align_bytes=64)
         for i, weight in enumerate(weights):
             nc.scalar.activation(out=scaled_ident[:, i, :], in_=ident[:], func=COPY, scale=weight)
-
-        def new_bank(number):
-            bank = psum.tile([P, H], F32, tag="bank%d" % number, bufs=1)
-            return bank
 
         def transpose_words(bank, words):
             for u in range(HALF):
@@ -115,6 +123,7 @@ def tile_sindylossmixin_pa_s_kernel(tc, x, k1, k2, coefficients, out):
             bank = new_bank(r)
             transpose_words(bank, x_words[:, r, :])
             nc.scalar.activation(out=in_pairs(y2T[:, r, :, :]), in_=by_row(bank), func=COPY, scale=2.0)
+        multiply_idly(2, P)
         for r in range(R):
             cols = slice(0, H if r < R - 1 else W)
             nc.vector.tensor_tensor(

from contextlib import ExitStack

import concourse.mybir as mybir
from concourse.masks import make_identity

F32 = mybir.dt.float32
BF16 = mybir.dt.bfloat16
U32 = mybir.dt.uint32
U8 = mybir.dt.uint8
FP8X4 = mybir.dt.float8_e4m3fn_x4
ALU = mybir.AluOpType
COPY = mybir.ActivationFunctionType.Copy

P = 128
B = 8
S = 49
H = 512
R = 3
Q = (S - 1) // R
PACK = 4
W = 384
HALF = 2

FLOPS = 2 * 2 * B * (S - 1) * H * H


def tile_sindylossmixin_pa_s_kernel(tc, x, k1, k2, coefficients, out):
    nc = tc.nc
    with ExitStack() as ctx:
        keep = ctx.enter_context(tc.tile_pool(name="keep", bufs=1))
        psum = ctx.enter_context(tc.psum_pool(name="psum", bufs=1))
        ctx.enter_context(tc.manual_schedule())

        x_sb = keep.tile([P, R + 1, H], BF16)
        k1_sb = keep.tile([P, R, H], BF16)
        k2_sb = keep.tile([P, R, H], BF16)
        c_sb = keep.tile([P, PACK, H], BF16)
        for first in (0, 2):
            nc.sync.dma_start(
                out=x_sb[:, first : first + 2, :].rearrange("p r h -> p (r h)"),
                in_=x[:, first // 2 : first // 2 + S - 1, :].rearrange("b (q r) h -> q b (r h)", r=R)[
                    :, :, first // 2 * H : (first // 2 + 2) * H
                ],
            )
        nc.sync.dma_start(
            out=k2_sb[:].rearrange("p r h -> p (r h)"),
            in_=k2.rearrange("(b q r) h -> q b (r h)", b=B, q=Q, r=R),
        )
        c_rows = coefficients.rearrange("(m t) j -> m t j", t=PACK)
        for h in range(HALF):
            nc.sync.dma_start(
                out=c_sb[:, HALF * h : HALF * (h + 1), :],
                in_=c_rows[:, HALF * h : HALF * (h + 1), :],
            )
        nc.sync.dma_start(
            out=k1_sb[:].rearrange("p r h -> p (r h)"),
            in_=k1.rearrange("(b q r) h -> q b (r h)", b=B, q=Q, r=R),
        )

        def new_bank(number):
            bank = psum.tile([P, H], F32, tag="bank%d" % number, bufs=1)
            return bank

        ident = keep.tile([P, P], F32)
        make_identity(nc, ident[:])

        warm = keep.tile([P, 2], F32)
        nc.vector.memset(warm[:, 0:1], 0.0)
        nc.scalar.activation(out=warm[:, 1:2], in_=warm[:, 0:1], func=COPY)

        idle_bank = new_bank(3)

        def multiply_idly(count, columns):
            for i in range(count):
                nc.tensor.matmul(idle_bank[:, 0:columns], ident[:], ident[:, 0:columns], start=True, stop=True)

        multiply_idly(4, 112)

        weights = [6.0, -6.0, 2.0, 1.0]
        scaled_ident = keep.tile([P, len(weights), P], BF16, align_bytes=64)
        for i, weight in enumerate(weights):
            nc.scalar.activation(out=scaled_ident[:, i, :], in_=ident[:], func=COPY, scale=weight)

        def transpose_words(bank, words):
            for u in range(HALF):
                nc.tensor.transpose(bank[:, u * P : (u + 1) * P], words[:, u : HALF * P : HALF], ident[:])

        def by_row(bank):
            return bank[:, 0 : HALF * P].bitcast(BF16).rearrange("p (u n e) -> p n u e", u=HALF, e=HALF)

        def in_pairs(grouped):
            return grouped.rearrange("p n (u e) -> p n u e", e=HALF)

        x_words = x_sb[:].bitcast(F32)
        k2_words = k2_sb[:].bitcast(F32)
        c_words = c_sb[:].bitcast(F32)
        y2T = keep.tile([P, R, P, PACK], BF16, align_bytes=64)
        aT = keep.tile([P, R, P, PACK], BF16, align_bytes=64)
        zT = keep.tile([P, R, P, PACK], BF16, align_bytes=64)
        cT = keep.tile([P, H, PACK], BF16, align_bytes=64)
        a_codes = keep.tile([P, R * P], U32, align_bytes=64)
        a_scales = keep.tile([P, R * P], U8, align_bytes=64)
        z_codes = keep.tile([P, R * P], U32, align_bytes=64)
        z_scales = keep.tile([P, R * P], U8, align_bytes=64)
        c_codes = keep.tile([P, H], U32, align_bytes=64)
        c_scales = keep.tile([P, H], U8, align_bytes=64)
        base = keep.tile([P, R, H], F32)
        result = keep.tile([P, R, H], F32)
        k1_sixth = keep.tile([P, R, H], F32)
        stages = keep.tile([P, H // 2], F32)

        def quantise(codes, scales, cols, grouped):
            nc.vector.quantize_mx(
                out=codes[:, cols].bitcast(FP8X4),
                scales=scales[:, cols],
                in_=grouped.rearrange("p n t -> p (n t)"),
            )

        def chunk(r):
            return slice(r * P, (r + 1) * P)

        for r in range(R):
            bank = new_bank(r)
            transpose_words(bank, x_words[:, r, :])
            nc.scalar.activation(out=in_pairs(y2T[:, r, :, :]), in_=by_row(bank), func=COPY, scale=2.0)
        multiply_idly(2, P)
        for r in range(R):
            cols = slice(0, H if r < R - 1 else W)
            nc.vector.tensor_tensor(
                out=base[:, r, cols], in0=x_sb[:, r, cols], in1=x_sb[:, r + 1, cols], op=ALU.subtract
            )

        def add_stage(r, cols, stage, factor):
            nc.vector.scalar_tensor_tensor(
                out=base[:, r, cols], in0=stage[:, r, cols], scalar=factor, in1=base[:, r, cols],
                op0=ALU.mult, op1=ALU.add,
            )

        add_stage(0, slice(0, H), k2_sb, 1.0 / 3.0)

        for r in range(R):
            bank = new_bank(4 + r)
            transpose_words(bank, k2_words[:, r, :])
            nc.vector.tensor_tensor(
                out=in_pairs(aT[:, r, :, :]), in0=by_row(bank), in1=in_pairs(y2T[:, r, :, :]), op=ALU.add
            )

        for t in range(PACK):
            bank = new_bank([7, 0, 1, 2][t])
            transpose_words(bank, c_words[:, t, :])
            nc.scalar.copy(
                out=cT[:, chunk(t), :].bitcast(F32),
                in_=bank[:, 0 : HALF * P].rearrange("p (u m) -> p m u", u=HALF),
            )

        known_bank = new_bank(3)
        rows = [x_sb[:, R - 1, W:H], x_sb[:, R, W:H], k2_sb[:, R - 1, W:H], k1_sb[:, R - 1, W:H]]

        def add_on_tensor(i):
            nc.tensor.matmul(
                known_bank[:, 0 : H - W], scaled_ident[:, i, :], rows[i],
                start=(i == 0), stop=(i == len(rows) - 1),
            )

        for i in range(len(rows) - 1):
            add_on_tensor(i)
        everything = slice(0, H)
        left = slice(0, H // 2)
        right = slice(H // 2, H)
        own = slice(0, W)
        for r, cols in ((1, everything), (0, right), (2, own)):
            nc.scalar.activation(
                out=k1_sixth[:, r, cols], in_=k1_sb[:, r, cols], func=COPY, scale=1.0 / 6.0
            )

        def add_k1_on_gpsimd(r, cols):
            nc.gpsimd.tensor_tensor(
                out=base[:, r, cols], in0=base[:, r, cols], in1=k1_sixth[:, r, cols], op=ALU.add
            )

        for r in range(R):
            quantise(a_codes, a_scales, chunk(r), aT[:, r, :, :])
        quantise(c_codes, c_scales, slice(0, 2 * P), cT[:, 0 : 2 * P, :])
        quantise(c_codes, c_scales, chunk(2), cT[:, chunk(2), :])
        quantise(c_codes, c_scales, chunk(3), cT[:, chunk(3), :])
        add_stage(1, everything, k2_sb, 1.0 / 3.0)
        add_k1_on_gpsimd(1, left)
        add_k1_on_gpsimd(1, right)
        add_k1_on_gpsimd(0, right)

        k3T_banks = []
        for r in range(R):
            bank = new_bank(4 + r)
            k3T_banks.append(bank)
            for t in range(PACK):
                nc.tensor.matmul_mx(
                    out=k3T_banks[r][:, chunk(t)],
                    lhsT=c_codes[:, chunk(t)].bitcast(FP8X4),
                    lhsT_scale=c_scales[:, chunk(t)],
                    rhs=a_codes[:, chunk(r)].bitcast(FP8X4),
                    rhs_scale=a_scales[:, chunk(r)],
                    start=True,
                    stop=True,
                )

        add_on_tensor(len(rows) - 1)
        nc.scalar.activation(
            out=base[:, R - 1, W:H], in_=known_bank[:, 0 : H - W], func=COPY, scale=1.0 / 6.0
        )

        for r in range(R + 1):
            if r < R:
                nc.vector.tensor_tensor(
                    out=zT[:, r, :, :],
                    in0=k3T_banks[r][:].rearrange("p (t n) -> p n t", t=PACK),
                    in1=y2T[:, r, :, :],
                    op=ALU.add,
                )
            if r == R - 1:
                add_stage(0, left, k1_sb, 1.0 / 6.0)
            if r == R:
                add_stage(2, own, k2_sb, 1.0 / 3.0)
            if r > 0:
                quantise(z_codes, z_scales, chunk(r - 1), zT[:, r - 1, :, :])

        def pass_over(bank, codes, scales, r, start, stop):
            nc.tensor.matmul_mx(
                out=bank[:],
                lhsT=codes[:, chunk(r)].bitcast(FP8X4),
                lhsT_scale=scales[:, chunk(r)],
                rhs=c_codes[:].bitcast(FP8X4),
                rhs_scale=c_scales[:],
                start=start,
                stop=stop,
            )

        sum_banks = []
        for r in range(R):
            bank = new_bank([7, 0, 1][r])
            sum_banks.append(bank)
            pass_over(bank, a_codes, a_scales, r, True, False)
            pass_over(bank, a_codes, a_scales, r, False, False)
            pass_over(bank, z_codes, z_scales, r, False, True)

        out_rows = out.rearrange("b (q r) h -> q b r h", r=R)

        def by_component(cols):
            return slice(cols.start // PACK, cols.stop // PACK)

        def sums(r, cols):
            return sum_banks[r][:].rearrange("p (t m) -> p m t", t=PACK)[:, by_component(cols), :]

        def finish(r, cols):
            nc.vector.scalar_tensor_tensor(
                out=result[:, r, cols].rearrange("p (m t) -> p m t", t=PACK),
                in0=sums(r, cols),
                scalar=1.0 / 12.0,
                in1=base[:, r, cols].rearrange("p (m t) -> p m t", t=PACK),
                op0=ALU.mult,
                op1=ALU.add,
            )

        def store(queue, r, cols):
            queue.dma_start(out=out_rows[:, :, r, cols], in_=result[:, r, cols])

        nc.scalar.activation(
            out=stages[:].rearrange("p (m t) -> p m t", t=PACK), in_=sums(0, right), func=COPY, scale=1.0 / 12.0
        )
        add_k1_on_gpsimd(2, own)
        nc.gpsimd.tensor_tensor(out=result[:, 0, right], in0=stages[:], in1=base[:, 0, right], op=ALU.add)
        finish(0, left)
        store(nc.sync, 0, left)
        finish(1, everything)
        store(nc.sync, 1, everything)
        finish(2, slice(W, H))
        store(nc.sync, 2, slice(W, H))
        store(nc.scalar, 0, right)
        finish(2, own)
        store(nc.sync, 2, own)
